import numpy as np
import ml_dtypes


def mxq(x, axis, fmt="e4m3"):
    dtype, down = {"e4m3": (ml_dtypes.float8_e4m3fn, 7), "e5m2": (ml_dtypes.float8_e5m2, 14)}[fmt]
    v = np.moveaxis(np.asarray(x, np.float32).astype(ml_dtypes.bfloat16).astype(np.float64), axis, -1)
    blocks = v.reshape(v.shape[:-1] + (-1, 32))
    amax = np.abs(blocks).max(-1, keepdims=True)
    byte = np.maximum(np.where(amax > 0, np.frexp(amax)[1] - 1 + 127, 0) - down, 1)
    scale = np.exp2(byte - 127.0)
    codes = (blocks / scale).astype(np.float32).astype(dtype).astype(np.float64)
    return np.moveaxis((codes * scale).reshape(v.shape), -1, axis)


WIDE = False


def mx_kscale(k):
    if not WIDE:
        return np.ones(k)
    levels = np.array([10, -10, 5, -5, 0])
    a = np.random.permutation(np.resize(levels, k // 512 * 4)).reshape(k // 512, 4)
    idx = np.arange(k)
    return np.exp2(a[idx // 512, idx % 128 // 32])


BF16 = ml_dtypes.bfloat16


def bf(x):
    return np.asarray(x, np.float32).astype(BF16)


def f64(x):
    return np.asarray(x).astype(np.float64)


IN_C, OUT_C, N, ND = 512, 512, 4096, 2


def sigmoid(v):
    return 1.0 / (1.0 + np.exp(-v))


def setup_inputs():
    s, t = mx_kscale(IN_C), mx_kscale(OUT_C)
    rn = np.random.standard_normal
    return {"x": bf(rn((IN_C, N)) * s[:, None]),
            "h_prev_dim0": bf(rn((OUT_C, N)) * t[:, None]),
            "h_prev_dim1": bf(rn((OUT_C, N)) * t[:, None]),
            "ct0": bf(rn((OUT_C, N)) * 0.65),
            "ct1": bf(rn((OUT_C, N)) * 0.65),
            "w_io": bf(rn((OUT_C, IN_C)) * 0.7 / np.sqrt(IN_C) / s[None, :]),
            "w_ho": bf(rn((OUT_C, OUT_C)) * 0.7 / np.sqrt(OUT_C) / t[None, :]),
            "b_o": bf(rn((OUT_C, 1)) * 0.5),
            "weighted_sum": bf(0.4 + 0.5 * np.random.random(ND))}


def reference(x, h_prev_dim0, h_prev_dim1, ct0, ct1, w_io, w_ho, b_o, weighted_sum):
    xo = mxq(f64(w_io), 1, "e4m3") @ mxq(f64(x), 0, "e4m3")
    who = mxq(f64(w_ho), 1, "e4m3")
    ws = f64(weighted_sum)

    def hidden(h_prev, c):
        o = sigmoid(xo + (who @ mxq(f64(h_prev), 0, "e4m3")) + f64(b_o))
        return o * np.tanh(f64(c))

    ht0 = hidden(h_prev_dim0, ct0)
    ht1 = hidden(h_prev_dim1, ct1)
    return ht0 * ws[0] + ht1 * ws[1]

@@ -1,0 +1,190 @@
+from contextlib import ExitStack
+
+import concourse.mybir as mybir
+from concourse.masks import make_identity
+
+FLOPS = 3 * 2 * 512 * 512 * 4096
+
+F32 = mybir.dt.float32
+BF16 = mybir.dt.bfloat16
+U32 = mybir.dt.uint32
+U8 = mybir.dt.uint8
+I32 = mybir.dt.int32
+FP8X4 = mybir.dt.float8_e4m3fn_x4
+ACT = mybir.ActivationFunctionType
+ALU = mybir.AluOpType
+
+P = 128
+PACK = 4
+CH = 512
+MT = CH // P
+NPOS = 4096
+UNIT = 512
+LOADW = 1024
+N_UNITS = NPOS // UNIT
+UPL = LOADW // UNIT
+SC_COLS = 384
+
+
+def tile_mdlstmcellweights_pb_t_kernel(
+    tc, x, h_prev_dim0, h_prev_dim1, ct0, ct1, w_io, w_ho, b_o, weighted_sum, out
+):
+    nc = tc.nc
+    with ExitStack() as ctx:
+        const = ctx.enter_context(tc.tile_pool(name="const", bufs=1))
+        rawp = ctx.enter_context(tc.tile_pool(name="rawp", bufs=2))
+        grpp = ctx.enter_context(tc.tile_pool(name="grpp", bufs=2))
+        codp = ctx.enter_context(tc.tile_pool(name="codp", bufs=3))
+        tp = ctx.enter_context(tc.tile_pool(name="tp", bufs=2))
+        op = ctx.enter_context(tc.tile_pool(name="op", bufs=2))
+        psum = ctx.enter_context(tc.psum_pool(name="psum", bufs=8))
+
+        mov_views = [a.rearrange("(t p) n -> p t n", p=P) for a in (x, h_prev_dim0, h_prev_dim1)]
+        ct_views = [a.rearrange("(m p) n -> p m n", p=P) for a in (ct0, ct1)]
+        out_v = out.rearrange("(m p) n -> p m n", p=P)
+
+        raw_mov = {}
+        raw_ct = {}
+
+        def load_mov(c, a):
+            r = rawp.tile([P, PACK, LOADW], BF16, name="rawm%d_%d" % (a, c), tag="rawm%d" % a)
+            nc.sync.dma_start(out=r[:], in_=mov_views[a][:, :, c * LOADW:(c + 1) * LOADW])
+            raw_mov[(c, a)] = r
+
+        def load_ct(c, d):
+            r = rawp.tile([P, MT, LOADW], BF16, name="rawc%d_%d" % (d, c), tag="rawc%d" % d)
+            nc.sync.dma_start(out=r[:], in_=ct_views[d][:, :, c * LOADW:(c + 1) * LOADW])
+            raw_ct[(c, d)] = r
+
+        warm = const.tile([P, 1], F32, name="warm")
+        nc.vector.memset(warm[:], 0.0)
+        nc.scalar.activation(out=warm[:], in_=warm[:], func=ACT.Sigmoid)
+
+        ident = const.tile([P, P], BF16, name="ident")
+        make_identity(nc, ident[:])
+
+        load_mov(0, 0)
+
+        w_raws = []
+        for wi, w in enumerate((w_io, w_ho)):
+            w_raw = const.tile([P, MT, CH], BF16, name="w_raw%d" % wi)
+            nc.sync.dma_start(out=w_raw[:], in_=w.rearrange("(m p) k -> p m k", p=P))
+            w_raws.append(w_raw)
+
+        b_rows = const.tile([P, P], BF16, name="b_rows")
+        nc.vector.memset(b_rows[:].bitcast(I32), 0)
+        nc.scalar.dma_start(out=b_rows[0:MT, :], in_=b_o.rearrange("(m p) one -> m (p one)", p=P))
+        ws_bf = const.tile([P, 2], BF16, name="ws_bf")
+        nc.scalar.dma_start(out=ws_bf[:], in_=weighted_sum.partition_broadcast(P))
+
+        load_mov(0, 1)
+        load_mov(0, 2)
+        load_ct(0, 0)
+        load_ct(0, 1)
+
+        w_codes = []
+        w_scales = []
+        for wi in range(2):
+            w_grp = const.tile([P, MT, P, PACK], BF16, name="w_grp%d" % wi, align_bytes=64)
+            for m in range(MT):
+                wt = psum.tile([P, PACK, P], BF16, name="wt%d_%d" % (wi, m), tag="bank")
+                for t in range(PACK):
+                    nc.tensor.transpose(wt[:, t, :], w_raws[wi][:, m, t * P:(t + 1) * P], ident[:])
+                nc.scalar.copy(out=w_grp[:, m], in_=wt[:].rearrange("p t o -> p o t"))
+            wc = const.tile([P, MT * P], U32, name="w_codes%d" % wi, align_bytes=64)
+            wsc = const.tile([P, MT * P], U8, name="w_scales%d" % wi, align_bytes=64)
+            nc.vector.quantize_mx(
+                out=wc[:].bitcast(FP8X4),
+                scales=wsc[:],
+                in_=w_grp[:].rearrange("p m o t -> p (m o t)"),
+            )
+            w_codes.append(wc)
+            w_scales.append(wsc)
+
+        b_ps = psum.tile([P, P], BF16, name="b_ps", tag="bank")
+        nc.tensor.transpose(b_ps[:], b_rows[:], ident[:])
+        b_sb = const.tile([P, MT], F32, name="b_sb")
+        nc.vector.tensor_copy(out=b_sb[:], in_=b_ps[:, 0:MT])
+        ws_sb = const.tile([P, 2], F32, name="ws_sb")
+        nc.vector.tensor_copy(out=ws_sb[:], in_=ws_bf[:])
+
+        codes = {}
+
+        def regroup(copy_fn, dst, src, c0, c1):
+            copy_fn(
+                out=dst[:, c0:c1, :].rearrange("p (c i) t -> p c t i", i=4),
+                in_=src[:, :, c0:c1].rearrange("p t (c i) -> p c t i", i=4),
+            )
+
+        def prep(u):
+            c, s = divmod(u, UPL)
+            grps = []
+            for a in range(3):
+                src = raw_mov[(c, a)][:, :, s * UNIT:(s + 1) * UNIT]
+                g = grpp.tile([P, UNIT, PACK], BF16, name="grp%d_%d" % (a, u), tag="grp%d" % a, align_bytes=64)
+                if a == 2 and SC_COLS > 0:
+                    regroup(nc.scalar.copy, g, src, UNIT - SC_COLS, UNIT)
+                    if SC_COLS < UNIT:
+                        regroup(nc.vector.tensor_copy, g, src, 0, UNIT - SC_COLS)
+                else:
+                    regroup(nc.vector.tensor_copy, g, src, 0, UNIT)
+                grps.append(g)
+            for a in range(3):
+                cd = codp.tile([P, UNIT], U32, name="cod%d_%d" % (a, u), tag="cod%d" % a, align_bytes=64)
+                sc = codp.tile([P, UNIT], U8, name="scl%d_%d" % (a, u), tag="scl%d" % a, align_bytes=64)
+                nc.vector.quantize_mx(
+                    out=cd[:].bitcast(FP8X4),
+                    scales=sc[:],
+                    in_=grps[a][:].rearrange("p n t -> p (n t)"),
+                )
+                codes[(u, a)] = (cd, sc)
+
+        def unit(u):
+            c, s = divmod(u, UPL)
+            ts = []
+            for d in range(2):
+                t = tp.tile([P, MT, UNIT], F32, name="t%d_%d" % (d, u), tag="t%d" % d)
+                nc.scalar.activation(out=t[:], in_=raw_ct[(c, d)][:, :, s * UNIT:(s + 1) * UNIT], func=ACT.Tanh)
+                ts.append(t)
+            os_ = []
+            xc, xs = codes[(u, 0)]
+            for d in range(2):
+                hc, hs = codes[(u, 1 + d)]
+                o = op.tile([P, MT, UNIT], F32, name="o%d_%d" % (d, u), tag="o%d" % d, bufs=(3 if d == 0 else 2))
+                for m in range(MT):
+                    acc = psum.tile([P, UNIT], F32, name="acc%d_%d_%d" % (u, d, m), tag="bank")
+                    mc = slice(m * P, (m + 1) * P)
+                    nc.tensor.matmul_mx(
+                        out=acc[:], lhsT=w_codes[0][:, mc].bitcast(FP8X4), lhsT_scale=w_scales[0][:, mc],
+                        rhs=xc[:].bitcast(FP8X4), rhs_scale=xs[:], start=True, stop=False,
+                    )
+                    nc.tensor.matmul_mx(
+                        out=acc[:], lhsT=w_codes[1][:, mc].bitcast(FP8X4), lhsT_scale=w_scales[1][:, mc],
+                        rhs=hc[:].bitcast(FP8X4), rhs_scale=hs[:], start=False, stop=True,
+                    )
+                    nc.scalar.activation(out=o[:, m, :], in_=acc[:], func=ACT.Sigmoid, bias=b_sb[:, m:m + 1], scale=1.0)
+                of = o[:].rearrange("p m n -> p (m n)")
+                nc.vector.scalar_tensor_tensor(
+                    out=of, in0=of, scalar=ws_sb[:, d:d + 1], in1=ts[d][:].rearrange("p m n -> p (m n)"),
+                    op0=ALU.mult, op1=ALU.mult,
+                )
+                os_.append(o)
+            o0f = os_[0][:].rearrange("p m n -> p (m n)")
+            nc.vector.tensor_tensor(out=o0f, in0=o0f, in1=os_[1][:].rearrange("p m n -> p (m n)"), op=ALU.add)
+            nc.sync.dma_start(out=out_v[:, :, u * UNIT:(u + 1) * UNIT], in_=os_[0][:])
+
+        def load_pair(c):
+            for a in range(3):
+                load_mov(c, a)
+            for d in range(2):
+                load_ct(c, d)
+
+        load_pair(1)
+        prep(0)
+        for u in range(N_UNITS):
+            if u + 1 < N_UNITS:
+                nxt = u + 1
+                if nxt % UPL == 0 and nxt // UPL + 1 < NPOS // LOADW:
+                    load_pair(nxt // UPL + 1)
+                prep(nxt)
+            unit(u)

@@ -20,10 +20,10 @@ CH = 512
 MT = CH // P
 NPOS = 4096
 UNIT = 512
-LOADW = 1024
 N_UNITS = NPOS // UNIT
-UPL = LOADW // UNIT
-SC_COLS = 384
+CHUNKS = (1, 1, 2, 2, 2)
+SHARE = (384, 384, 384, 384, 384, 384, 384, 384)
+PINNED = False
 
 
 def tile_mdlstmcellweights_pb_t_kernel(
@@ -38,52 +38,138 @@ def tile_mdlstmcellweights_pb_t_kernel(
         tp = ctx.enter_context(tc.tile_pool(name="tp", bufs=2))
         op = ctx.enter_context(tc.tile_pool(name="op", bufs=2))
         psum = ctx.enter_context(tc.psum_pool(name="psum", bufs=8))
+        if PINNED:
+            ctx.enter_context(tc.manual_schedule())
 
         mov_views = [a.rearrange("(t p) n -> p t n", p=P) for a in (x, h_prev_dim0, h_prev_dim1)]
         ct_views = [a.rearrange("(m p) n -> p m n", p=P) for a in (ct0, ct1)]
         out_v = out.rearrange("(m p) n -> p m n", p=P)
 
+        chunk_of = []
+        chunk_start = []
+        for c, w in enumerate(CHUNKS):
+            chunk_start.append(len(chunk_of) * UNIT)
+            for i in range(w):
+                chunk_of.append((c, i))
+        n_chunks = len(CHUNKS)
+
+        def last_of_chunk(u):
+            return u + 1 >= N_UNITS or chunk_of[u + 1][0] != chunk_of[u][0]
+
         raw_mov = {}
         raw_ct = {}
+        grp = {}
+        codes = {}
+        tt = {}
+        oo = {}
 
-        def load_mov(c, a):
-            r = rawp.tile([P, PACK, LOADW], BF16, name="rawm%d_%d" % (a, c), tag="rawm%d" % a)
-            nc.sync.dma_start(out=r[:], in_=mov_views[a][:, :, c * LOADW:(c + 1) * LOADW])
+        def ldm(c, a):
+            w = CHUNKS[c] * UNIT
+            r = rawp.tile([P, PACK, w], BF16, name="rawm%d_%d" % (a, c), tag="rawm%d" % a)
+            nc.sync.dma_start(out=r[:], in_=mov_views[a][:, :, chunk_start[c]:chunk_start[c] + w])
             raw_mov[(c, a)] = r
 
-        def load_ct(c, d):
-            r = rawp.tile([P, MT, LOADW], BF16, name="rawc%d_%d" % (d, c), tag="rawc%d" % d)
-            nc.sync.dma_start(out=r[:], in_=ct_views[d][:, :, c * LOADW:(c + 1) * LOADW])
+        def ldc(c, d):
+            w = CHUNKS[c] * UNIT
+            r = rawp.tile([P, MT, w], BF16, name="rawc%d_%d" % (d, c), tag="rawc%d" % d)
+            nc.sync.dma_start(out=r[:], in_=ct_views[d][:, :, chunk_start[c]:chunk_start[c] + w])
             raw_ct[(c, d)] = r
+
+        def rg(copy_fn, u, a, c0, c1):
+            if c1 <= c0:
+                return
+            if (u, a) not in grp:
+                grp[(u, a)] = grpp.tile([P, UNIT, PACK], BF16, name="grp%d_%d" % (a, u), tag="grp%d" % a, align_bytes=64)
+            c, s = chunk_of[u]
+            src = raw_mov[(c, a)][:, :, s * UNIT + c0:s * UNIT + c1]
+            copy_fn(
+                out=grp[(u, a)][:, c0:c1, :].rearrange("p (c i) t -> p c t i", i=4),
+                in_=src.rearrange("p t (c i) -> p c t i", i=4),
+            )
+
+        def rgv(u, a, c0=0, c1=UNIT):
+            rg(nc.vector.tensor_copy, u, a, c0, c1)
+
+        def rgs(u, a, c0, c1):
+            rg(nc.scalar.copy, u, a, c0, c1)
+
+        def q(u, a):
+            cd = codp.tile([P, UNIT], U32, name="cod%d_%d" % (a, u), tag="cod%d" % a, align_bytes=64)
+            sc = codp.tile([P, UNIT], U8, name="scl%d_%d" % (a, u), tag="scl%d" % a, align_bytes=64)
+            nc.vector.quantize_mx(
+                out=cd[:].bitcast(FP8X4), scales=sc[:], in_=grp[(u, a)][:].rearrange("p n t -> p (n t)")
+            )
+            codes[(u, a)] = (cd, sc)
+
+        def tanh(u, d, m0=0, m1=MT):
+            if (u, d) not in tt:
+                tt[(u, d)] = tp.tile([P, MT, UNIT], F32, name="t%d_%d" % (d, u), tag="t%d" % d)
+            c, s = chunk_of[u]
+            nc.scalar.activation(
+                out=tt[(u, d)][:, m0:m1, :], in_=raw_ct[(c, d)][:, m0:m1, s * UNIT:(s + 1) * UNIT], func=ACT.Tanh
+            )
+
+        def mmsig(u, d, m):
+            if (u, d) not in oo:
+                oo[(u, d)] = op.tile([P, MT, UNIT], F32, name="o%d_%d" % (d, u), tag="o%d" % d, bufs=(3 if d == 0 else 2))
+            xc, xs = codes[(u, 0)]
+            hc, hs = codes[(u, 1 + d)]
+            acc = psum.tile([P, UNIT], F32, name="acc%d_%d_%d" % (u, d, m), tag="bank")
+            mc = slice(m * P, (m + 1) * P)
+            nc.tensor.matmul_mx(
+                out=acc[:], lhsT=w_codes[0][:, mc].bitcast(FP8X4), lhsT_scale=w_scales[0][:, mc],
+                rhs=xc[:].bitcast(FP8X4), rhs_scale=xs[:], start=True, stop=False,
+            )
+            nc.tensor.matmul_mx(
+                out=acc[:], lhsT=w_codes[1][:, mc].bitcast(FP8X4), lhsT_scale=w_scales[1][:, mc],
+                rhs=hc[:].bitcast(FP8X4), rhs_scale=hs[:], start=False, stop=True,
+            )
+            nc.scalar.activation(out=oo[(u, d)][:, m, :], in_=acc[:], func=ACT.Sigmoid, bias=b_sb[:, m:m + 1], scale=1.0)
+
+        def flat(t, m0, m1):
+            return t[:, m0:m1, :].rearrange("p m n -> p (m n)")
+
+        def prod(u, d, m0=0, m1=MT):
+            of = flat(oo[(u, d)], m0, m1)
+            nc.vector.scalar_tensor_tensor(
+                out=of, in0=of, scalar=ws_sb[:, d:d + 1], in1=flat(tt[(u, d)], m0, m1), op0=ALU.mult, op1=ALU.mult
+            )
+
+        def add(u, m0=0, m1=MT):
+            of = flat(oo[(u, 0)], m0, m1)
+            nc.vector.tensor_tensor(out=of, in0=of, in1=flat(oo[(u, 1)], m0, m1), op=ALU.add)
+
+        def st(u, m0=0, m1=MT):
+            nc.sync.dma_start(out=out_v[:, m0:m1, u * UNIT:(u + 1) * UNIT], in_=oo[(u, 0)][:, m0:m1, :])
 
         warm = const.tile([P, 1], F32, name="warm")
         nc.vector.memset(warm[:], 0.0)
         nc.scalar.activation(out=warm[:], in_=warm[:], func=ACT.Sigmoid)
-
+        b_rows = const.tile([P, P], BF16, name="b_rows")
+        nc.vector.memset(b_rows[:].bitcast(I32), 0)
+        nc.scalar.dma_start(out=b_rows[0:MT, :], in_=b_o.rearrange("(m p) one -> m (p one)", p=P))
+        ws_bf = const.tile([P, 2], BF16, name="ws_bf")
+        nc.scalar.dma_start(out=ws_bf[:], in_=weighted_sum.partition_broadcast(P))
         ident = const.tile([P, P], BF16, name="ident")
         make_identity(nc, ident[:])
-
-        load_mov(0, 0)
 
         w_raws = []
         for wi, w in enumerate((w_io, w_ho)):
             w_raw = const.tile([P, MT, CH], BF16, name="w_raw%d" % wi)
             nc.sync.dma_start(out=w_raw[:], in_=w.rearrange("(m p) k -> p m k", p=P))
             w_raws.append(w_raw)
+        for a in range(3):
+            ldm(0, a)
+        for d in range(2):
+            ldc(0, d)
+        for a in range(3):
+            ldm(1, a)
+        for d in range(2):
+            ldc(1, d)
+        next_m = 2
+        next_c = 2
 
-        b_rows = const.tile([P, P], BF16, name="b_rows")
-        nc.vector.memset(b_rows[:].bitcast(I32), 0)
-        nc.scalar.dma_start(out=b_rows[0:MT, :], in_=b_o.rearrange("(m p) one -> m (p one)", p=P))
-        ws_bf = const.tile([P, 2], BF16, name="ws_bf")
-        nc.scalar.dma_start(out=ws_bf[:], in_=weighted_sum.partition_broadcast(P))
-
-        load_mov(0, 1)
-        load_mov(0, 2)
-        load_ct(0, 0)
-        load_ct(0, 1)
-
-        w_codes = []
-        w_scales = []
+        w_grps = []
         for wi in range(2):
             w_grp = const.tile([P, MT, P, PACK], BF16, name="w_grp%d" % wi, align_bytes=64)
             for m in range(MT):
@@ -91,100 +177,79 @@ def tile_mdlstmcellweights_pb_t_kernel(
                 for t in range(PACK):
                     nc.tensor.transpose(wt[:, t, :], w_raws[wi][:, m, t * P:(t + 1) * P], ident[:])
                 nc.scalar.copy(out=w_grp[:, m], in_=wt[:].rearrange("p t o -> p o t"))
+            w_grps.append(w_grp)
+        b_ps = psum.tile([P, P], BF16, name="b_ps", tag="bank")
+        nc.tensor.transpose(b_ps[:], b_rows[:], ident[:])
+
+        w_codes = []
+        w_scales = []
+
+        def wq(wi):
             wc = const.tile([P, MT * P], U32, name="w_codes%d" % wi, align_bytes=64)
             wsc = const.tile([P, MT * P], U8, name="w_scales%d" % wi, align_bytes=64)
             nc.vector.quantize_mx(
-                out=wc[:].bitcast(FP8X4),
-                scales=wsc[:],
-                in_=w_grp[:].rearrange("p m o t -> p (m o t)"),
+                out=wc[:].bitcast(FP8X4), scales=wsc[:], in_=w_grps[wi][:].rearrange("p m o t -> p (m o t)")
             )
             w_codes.append(wc)
             w_scales.append(wsc)
 
-        b_ps = psum.tile([P, P], BF16, name="b_ps", tag="bank")
-        nc.tensor.transpose(b_ps[:], b_rows[:], ident[:])
+        wq(0)
+        rgv(0, 0)
+        wq(1)
+        rgv(0, 1)
+        q(0, 0)
         b_sb = const.tile([P, MT], F32, name="b_sb")
         nc.vector.tensor_copy(out=b_sb[:], in_=b_ps[:, 0:MT])
         ws_sb = const.tile([P, 2], F32, name="ws_sb")
         nc.vector.tensor_copy(out=ws_sb[:], in_=ws_bf[:])
-
-        codes = {}
-
-        def regroup(copy_fn, dst, src, c0, c1):
-            copy_fn(
-                out=dst[:, c0:c1, :].rearrange("p (c i) t -> p c t i", i=4),
-                in_=src[:, :, c0:c1].rearrange("p t (c i) -> p c t i", i=4),
-            )
-
-        def prep(u):
-            c, s = divmod(u, UPL)
-            grps = []
+        rgs(0, 2, UNIT - SHARE[0], UNIT)
+        rgv(0, 2, 0, UNIT - SHARE[0])
+        q(0, 1)
+        q(0, 2)
+        if last_of_chunk(0) and next_m < n_chunks:
             for a in range(3):
-                src = raw_mov[(c, a)][:, :, s * UNIT:(s + 1) * UNIT]
-                g = grpp.tile([P, UNIT, PACK], BF16, name="grp%d_%d" % (a, u), tag="grp%d" % a, align_bytes=64)
-                if a == 2 and SC_COLS > 0:
-                    regroup(nc.scalar.copy, g, src, UNIT - SC_COLS, UNIT)
-                    if SC_COLS < UNIT:
-                        regroup(nc.vector.tensor_copy, g, src, 0, UNIT - SC_COLS)
-                else:
-                    regroup(nc.vector.tensor_copy, g, src, 0, UNIT)
-                grps.append(g)
-            for a in range(3):
-                cd = codp.tile([P, UNIT], U32, name="cod%d_%d" % (a, u), tag="cod%d" % a, align_bytes=64)
-                sc = codp.tile([P, UNIT], U8, name="scl%d_%d" % (a, u), tag="scl%d" % a, align_bytes=64)
-                nc.vector.quantize_mx(
-                    out=cd[:].bitcast(FP8X4),
-                    scales=sc[:],
-                    in_=grps[a][:].rearrange("p n t -> p (n t)"),
-                )
-                codes[(u, a)] = (cd, sc)
+                ldm(next_m, a)
+            next_m += 1
+        tanh(0, 0)
 
-        def unit(u):
-            c, s = divmod(u, UPL)
-            ts = []
-            for d in range(2):
-                t = tp.tile([P, MT, UNIT], F32, name="t%d_%d" % (d, u), tag="t%d" % d)
-                nc.scalar.activation(out=t[:], in_=raw_ct[(c, d)][:, :, s * UNIT:(s + 1) * UNIT], func=ACT.Tanh)
-                ts.append(t)
-            os_ = []
-            xc, xs = codes[(u, 0)]
-            for d in range(2):
-                hc, hs = codes[(u, 1 + d)]
-                o = op.tile([P, MT, UNIT], F32, name="o%d_%d" % (d, u), tag="o%d" % d, bufs=(3 if d == 0 else 2))
-                for m in range(MT):
-                    acc = psum.tile([P, UNIT], F32, name="acc%d_%d_%d" % (u, d, m), tag="bank")
-                    mc = slice(m * P, (m + 1) * P)
-                    nc.tensor.matmul_mx(
-                        out=acc[:], lhsT=w_codes[0][:, mc].bitcast(FP8X4), lhsT_scale=w_scales[0][:, mc],
-                        rhs=xc[:].bitcast(FP8X4), rhs_scale=xs[:], start=True, stop=False,
-                    )
-                    nc.tensor.matmul_mx(
-                        out=acc[:], lhsT=w_codes[1][:, mc].bitcast(FP8X4), lhsT_scale=w_scales[1][:, mc],
-                        rhs=hc[:].bitcast(FP8X4), rhs_scale=hs[:], start=False, stop=True,
-                    )
-                    nc.scalar.activation(out=o[:, m, :], in_=acc[:], func=ACT.Sigmoid, bias=b_sb[:, m:m + 1], scale=1.0)
-                of = o[:].rearrange("p m n -> p (m n)")
-                nc.vector.scalar_tensor_tensor(
-                    out=of, in0=of, scalar=ws_sb[:, d:d + 1], in1=ts[d][:].rearrange("p m n -> p (m n)"),
-                    op0=ALU.mult, op1=ALU.mult,
-                )
-                os_.append(o)
-            o0f = os_[0][:].rearrange("p m n -> p (m n)")
-            nc.vector.tensor_tensor(out=o0f, in0=o0f, in1=os_[1][:].rearrange("p m n -> p (m n)"), op=ALU.add)
-            nc.sync.dma_start(out=out_v[:, :, u * UNIT:(u + 1) * UNIT], in_=os_[0][:])
-
-        def load_pair(c):
-            for a in range(3):
-                load_mov(c, a)
-            for d in range(2):
-                load_ct(c, d)
-
-        load_pair(1)
-        prep(0)
         for u in range(N_UNITS):
-            if u + 1 < N_UNITS:
-                nxt = u + 1
-                if nxt % UPL == 0 and nxt // UPL + 1 < NPOS // LOADW:
-                    load_pair(nxt // UPL + 1)
-                prep(nxt)
-            unit(u)
+            v = u + 1
+            has = v < N_UNITS
+            last = u == N_UNITS - 1
+            if has:
+                rgv(v, 0)
+                rgv(v, 1)
+                q(v, 0)
+                rgv(v, 2, 0, UNIT - SHARE[v])
+                q(v, 1)
+            for m in range(MT):
+                mmsig(u, 0, m)
+            if has:
+                rgs(v, 2, UNIT - SHARE[v], UNIT)
+            if not last:
+                tanh(u, 1)
+                if last_of_chunk(u) and next_c < n_chunks:
+                    for d in range(2):
+                        ldc(next_c, d)
+                    next_c += 1
+            prod(u, 0)
+            if has:
+                q(v, 2)
+                if last_of_chunk(v) and next_m < n_chunks:
+                    for a in range(3):
+                        ldm(next_m, a)
+                    next_m += 1
+            if not last:
+                for m in range(MT):
+                    mmsig(u, 1, m)
+                tanh(v, 0)
+                prod(u, 1)
+                add(u)
+                st(u)
+            else:
+                for m in range(MT):
+                    tanh(u, 1, m, m + 1)
+                    mmsig(u, 1, m)
+                    prod(u, 1, m, m + 1)
+                    add(u, m, m + 1)
+                    st(u, m, m + 1)

@@ -23,7 +23,6 @@ UNIT = 512
 N_UNITS = NPOS // UNIT
 CHUNKS = (1, 1, 2, 2, 2)
 SHARE = (384, 384, 384, 384, 384, 384, 384, 384)
-PINNED = False
 
 
 def tile_mdlstmcellweights_pb_t_kernel(
@@ -36,10 +35,7 @@ def tile_mdlstmcellweights_pb_t_kernel(
         grpp = ctx.enter_context(tc.tile_pool(name="grpp", bufs=2))
         codp = ctx.enter_context(tc.tile_pool(name="codp", bufs=3))
         tp = ctx.enter_context(tc.tile_pool(name="tp", bufs=2))
-        op = ctx.enter_context(tc.tile_pool(name="op", bufs=2))
         psum = ctx.enter_context(tc.psum_pool(name="psum", bufs=8))
-        if PINNED:
-            ctx.enter_context(tc.manual_schedule())
 
         mov_views = [a.rearrange("(t p) n -> p t n", p=P) for a in (x, h_prev_dim0, h_prev_dim1)]
         ct_views = [a.rearrange("(m p) n -> p m n", p=P) for a in (ct0, ct1)]
@@ -153,49 +149,52 @@ def tile_mdlstmcellweights_pb_t_kernel(
         ident = const.tile([P, P], BF16, name="ident")
         make_identity(nc, ident[:])
 
-        w_raws = []
-        for wi, w in enumerate((w_io, w_ho)):
-            w_raw = const.tile([P, MT, CH], BF16, name="w_raw%d" % wi)
-            nc.sync.dma_start(out=w_raw[:], in_=w.rearrange("(m p) k -> p m k", p=P))
-            w_raws.append(w_raw)
-        for a in range(3):
-            ldm(0, a)
-        for d in range(2):
-            ldc(0, d)
-        for a in range(3):
-            ldm(1, a)
-        for d in range(2):
-            ldc(1, d)
-        next_m = 2
-        next_c = 2
+        with tc.tile_pool(name="wtmp", bufs=1) as wtmp:
+            w_raws = []
+            for wi in range(2):
+                w_raws.append(wtmp.tile([P, MT, CH], BF16, name="w_raw%d" % wi))
+            nc.sync.dma_start(out=w_raws[0][:], in_=w_io.rearrange("(m p) k -> p m k", p=P))
+            ldc(0, 0)
+            ldm(0, 0)
+            nc.sync.dma_start(out=w_raws[1][:], in_=w_ho.rearrange("(m p) k -> p m k", p=P))
+            ldm(0, 1)
+            ldc(0, 1)
+            ldm(0, 2)
+            for a in range(3):
+                ldm(1, a)
+            for d in range(2):
+                ldc(1, d)
+            next_m = 2
+            next_c = 2
 
-        w_grps = []
-        for wi in range(2):
-            w_grp = const.tile([P, MT, P, PACK], BF16, name="w_grp%d" % wi, align_bytes=64)
-            for m in range(MT):
-                wt = psum.tile([P, PACK, P], BF16, name="wt%d_%d" % (wi, m), tag="bank")
-                for t in range(PACK):
-                    nc.tensor.transpose(wt[:, t, :], w_raws[wi][:, m, t * P:(t + 1) * P], ident[:])
-                nc.scalar.copy(out=w_grp[:, m], in_=wt[:].rearrange("p t o -> p o t"))
-            w_grps.append(w_grp)
-        b_ps = psum.tile([P, P], BF16, name="b_ps", tag="bank")
-        nc.tensor.transpose(b_ps[:], b_rows[:], ident[:])
+            w_grps = []
+            for wi in range(2):
+                w_grp = wtmp.tile([P, MT, P, PACK], BF16, name="w_grp%d" % wi, align_bytes=64)
+                for m in range(MT):
+                    wt = psum.tile([P, PACK, P], BF16, name="wt%d_%d" % (wi, m), tag="bank")
+                    for t in range(PACK):
+                        nc.tensor.transpose(wt[:, t, :], w_raws[wi][:, m, t * P:(t + 1) * P], ident[:])
+                    nc.scalar.copy(out=w_grp[:, m], in_=wt[:].rearrange("p t o -> p o t"))
+                w_grps.append(w_grp)
+            b_ps = psum.tile([P, P], BF16, name="b_ps", tag="bank")
+            nc.tensor.transpose(b_ps[:], b_rows[:], ident[:])
 
-        w_codes = []
-        w_scales = []
+            w_codes = []
+            w_scales = []
 
-        def wq(wi):
-            wc = const.tile([P, MT * P], U32, name="w_codes%d" % wi, align_bytes=64)
-            wsc = const.tile([P, MT * P], U8, name="w_scales%d" % wi, align_bytes=64)
-            nc.vector.quantize_mx(
-                out=wc[:].bitcast(FP8X4), scales=wsc[:], in_=w_grps[wi][:].rearrange("p m o t -> p (m o t)")
-            )
-            w_codes.append(wc)
-            w_scales.append(wsc)
+            def wq(wi):
+                wc = const.tile([P, MT * P], U32, name="w_codes%d" % wi, align_bytes=64)
+                wsc = const.tile([P, MT * P], U8, name="w_scales%d" % wi, align_bytes=64)
+                nc.vector.quantize_mx(
+                    out=wc[:].bitcast(FP8X4), scales=wsc[:], in_=w_grps[wi][:].rearrange("p m o t -> p (m o t)")
+                )
+                w_codes.append(wc)
+                w_scales.append(wsc)
 
-        wq(0)
-        rgv(0, 0)
-        wq(1)
+            wq(0)
+            rgv(0, 0)
+            wq(1)
+        op = ctx.enter_context(tc.tile_pool(name="op", bufs=2))
         rgv(0, 1)
         q(0, 0)
         b_sb = const.tile([P, MT], F32, name="b_sb")
@@ -222,8 +221,9 @@ def tile_mdlstmcellweights_pb_t_kernel(
                 q(v, 0)
                 rgv(v, 2, 0, UNIT - SHARE[v])
                 q(v, 1)
-            for m in range(MT):
-                mmsig(u, 0, m)
+            if not last:
+                for m in range(MT):
+                    mmsig(u, 0, m)
             if has:
                 rgs(v, 2, UNIT - SHARE[v], UNIT)
             if not last:
@@ -232,7 +232,8 @@ def tile_mdlstmcellweights_pb_t_kernel(
                     for d in range(2):
                         ldc(next_c, d)
                     next_c += 1
-            prod(u, 0)
+            if not last:
+                prod(u, 0)
             if has:
                 q(v, 2)
                 if last_of_chunk(v) and next_m < n_chunks:
@@ -242,12 +243,16 @@ def tile_mdlstmcellweights_pb_t_kernel(
             if not last:
                 for m in range(MT):
                     mmsig(u, 1, m)
-                tanh(v, 0)
+                if v < N_UNITS - 1:
+                    tanh(v, 0)
                 prod(u, 1)
                 add(u)
                 st(u)
             else:
                 for m in range(MT):
+                    tanh(u, 0, m, m + 1)
+                    mmsig(u, 0, m)
+                    prod(u, 0, m, m + 1)
                     tanh(u, 1, m, m + 1)
                     mmsig(u, 1, m)
                     prod(u, 1, m, m + 1)

@@ -22,7 +22,7 @@ NPOS = 4096
 UNIT = 512
 N_UNITS = NPOS // UNIT
 CHUNKS = (1, 1, 2, 2, 2)
-SHARE = (384, 384, 384, 384, 384, 384, 384, 384)
+SHARE = (512, 512, 512, 512, 512, 512, 512, 512)
 
 
 def tile_mdlstmcellweights_pb_t_kernel(

@@ -87,7 +87,20 @@ def tile_mdlstmcellweights_pb_t_kernel(
             rg(nc.vector.tensor_copy, u, a, c0, c1)
 
         def rgs(u, a, c0, c1):
-            rg(nc.scalar.copy, u, a, c0, c1)
+            assert c0 == 0 and c1 == UNIT
+            grp[(u, a)] = grpp.tile([P, UNIT, PACK], BF16, name="grp%d_%d" % (a, u), tag="grp%d" % a, align_bytes=64)
+            c, s = chunk_of[u]
+            for hf in range(2):
+                bank = psum.tile([P, 2 * P * PACK], BF16, name="rgb%d_%d_%d" % (a, u, hf), tag="bank")
+                for qq in range(2):
+                    n0 = s * UNIT + (2 * hf + qq) * P
+                    nc.tensor.matmul(
+                        out=bank[:, qq * P * PACK:(qq + 1) * P * PACK].rearrange("p (n t) -> p t n", t=PACK),
+                        lhsT=ident[:], rhs=raw_mov[(c, a)][:, :, n0:n0 + P], start=True, stop=True,
+                    )
+                nc.scalar.copy(
+                    out=grp[(u, a)][:, 2 * hf * P:2 * (hf + 1) * P, :].rearrange("p n t -> p (n t)"), in_=bank[:]
+                )
 
         def q(u, a):
             cd = codp.tile([P, UNIT], U32, name="cod%d_%d" % (a, u), tag="cod%d" % a, align_bytes=64)

@@ -22,7 +22,8 @@ NPOS = 4096
 UNIT = 512
 N_UNITS = NPOS // UNIT
 CHUNKS = (1, 1, 2, 2, 2)
-SHARE = (512, 512, 512, 512, 512, 512, 512, 512)
+EXTRA = 64
+EXTRA_FROM = 2
 
 
 def tile_mdlstmcellweights_pb_t_kernel(
@@ -52,18 +53,26 @@ def tile_mdlstmcellweights_pb_t_kernel(
         def last_of_chunk(u):
             return u + 1 >= N_UNITS or chunk_of[u + 1][0] != chunk_of[u][0]
 
-        raw_mov = {}
+        raw_xh = {}
+        raw_h1 = {}
         raw_ct = {}
-        grp = {}
-        codes = {}
+        grp_xh = {}
+        grp_h1 = {}
+        cod_xh = {}
+        cod_h1 = {}
         tt = {}
         oo = {}
 
         def ldm(c, a):
             w = CHUNKS[c] * UNIT
-            r = rawp.tile([P, PACK, w], BF16, name="rawm%d_%d" % (a, c), tag="rawm%d" % a)
-            nc.sync.dma_start(out=r[:], in_=mov_views[a][:, :, chunk_start[c]:chunk_start[c] + w])
-            raw_mov[(c, a)] = r
+            src = mov_views[a][:, :, chunk_start[c]:chunk_start[c] + w]
+            if a == 2:
+                raw_h1[c] = rawp.tile([P, PACK, w], BF16, name="rawh1_%d" % c, tag="rawh1")
+                nc.sync.dma_start(out=raw_h1[c][:], in_=src)
+            else:
+                if c not in raw_xh:
+                    raw_xh[c] = rawp.tile([P, 2, PACK, w], BF16, name="rawxh_%d" % c, tag="rawxh")
+                nc.sync.dma_start(out=raw_xh[c][:, a], in_=src)
 
         def ldc(c, d):
             w = CHUNKS[c] * UNIT
@@ -71,44 +80,78 @@ def tile_mdlstmcellweights_pb_t_kernel(
             nc.sync.dma_start(out=r[:], in_=ct_views[d][:, :, chunk_start[c]:chunk_start[c] + w])
             raw_ct[(c, d)] = r
 
-        def rg(copy_fn, u, a, c0, c1):
-            if c1 <= c0:
-                return
-            if (u, a) not in grp:
-                grp[(u, a)] = grpp.tile([P, UNIT, PACK], BF16, name="grp%d_%d" % (a, u), tag="grp%d" % a, align_bytes=64)
+        def extra(u):
+            return EXTRA if u >= EXTRA_FROM else 0
+
+        def new_xh(u):
+            grp_xh[u] = grpp.tile([P, 2, UNIT, PACK], BF16, name="grpxh_%d" % u, tag="grpxh", align_bytes=64)
+            cd = codp.tile([P, 2, UNIT], U32, name="codxh_%d" % u, tag="codxh", align_bytes=64)
+            sc = codp.tile([P, 2, UNIT], U8, name="sclxh_%d" % u, tag="sclxh", align_bytes=64)
+            cod_xh[u] = (cd, sc)
+
+        def rg_one(u, a):
             c, s = chunk_of[u]
-            src = raw_mov[(c, a)][:, :, s * UNIT + c0:s * UNIT + c1]
-            copy_fn(
-                out=grp[(u, a)][:, c0:c1, :].rearrange("p (c i) t -> p c t i", i=4),
-                in_=src.rearrange("p t (c i) -> p c t i", i=4),
+            nc.vector.tensor_copy(
+                out=grp_xh[u][:, a].rearrange("p (c i) t -> p c t i", i=4),
+                in_=raw_xh[c][:, a, :, s * UNIT:(s + 1) * UNIT].rearrange("p t (c i) -> p c t i", i=4),
             )
 
-        def rgv(u, a, c0=0, c1=UNIT):
-            rg(nc.vector.tensor_copy, u, a, c0, c1)
+        def rg_both(u):
+            c, s = chunk_of[u]
+            e = extra(u)
+            nc.vector.tensor_copy(
+                out=grp_xh[u][:, :, e:, :].rearrange("p a (c i) t -> p a c t i", i=4),
+                in_=raw_xh[c][:, :, :, s * UNIT + e:(s + 1) * UNIT].rearrange("p a t (c i) -> p a c t i", i=4),
+            )
 
-        def rgs(u, a, c0, c1):
-            assert c0 == 0 and c1 == UNIT
-            grp[(u, a)] = grpp.tile([P, UNIT, PACK], BF16, name="grp%d_%d" % (a, u), tag="grp%d" % a, align_bytes=64)
+        def q_one(u, a):
+            cd, sc = cod_xh[u]
+            nc.vector.quantize_mx(
+                out=cd[:, a].bitcast(FP8X4), scales=sc[:, a], in_=grp_xh[u][:, a].rearrange("p n t -> p (n t)")
+            )
+
+        def q_both(u):
+            cd, sc = cod_xh[u]
+            nc.vector.quantize_mx(
+                out=cd[:].rearrange("p a n -> p (a n)").bitcast(FP8X4),
+                scales=sc[:].rearrange("p a n -> p (a n)"),
+                in_=grp_xh[u][:].rearrange("p a n t -> p (a n t)"),
+            )
+
+        def pe_regroup(bank_cols, raw_tn):
+            nc.tensor.matmul(
+                out=bank_cols.rearrange("p (n t) -> p t n", t=PACK), lhsT=ident[:], rhs=raw_tn, start=True, stop=True
+            )
+
+        def rg_h1(u):
+            grp_h1[u] = grpp.tile([P, UNIT, PACK], BF16, name="grph1_%d" % u, tag="grph1", align_bytes=64)
             c, s = chunk_of[u]
             for hf in range(2):
-                bank = psum.tile([P, 2 * P * PACK], BF16, name="rgb%d_%d_%d" % (a, u, hf), tag="bank")
+                bank = psum.tile([P, 2 * P * PACK], BF16, name="rgb_%d_%d" % (u, hf), tag="bank")
                 for qq in range(2):
                     n0 = s * UNIT + (2 * hf + qq) * P
-                    nc.tensor.matmul(
-                        out=bank[:, qq * P * PACK:(qq + 1) * P * PACK].rearrange("p (n t) -> p t n", t=PACK),
-                        lhsT=ident[:], rhs=raw_mov[(c, a)][:, :, n0:n0 + P], start=True, stop=True,
-                    )
+                    pe_regroup(bank[:, qq * P * PACK:(qq + 1) * P * PACK], raw_h1[c][:, :, n0:n0 + P])
                 nc.scalar.copy(
-                    out=grp[(u, a)][:, 2 * hf * P:2 * (hf + 1) * P, :].rearrange("p n t -> p (n t)"), in_=bank[:]
+                    out=grp_h1[u][:, 2 * hf * P:2 * (hf + 1) * P, :].rearrange("p n t -> p (n t)"), in_=bank[:]
                 )
 
-        def q(u, a):
-            cd = codp.tile([P, UNIT], U32, name="cod%d_%d" % (a, u), tag="cod%d" % a, align_bytes=64)
-            sc = codp.tile([P, UNIT], U8, name="scl%d_%d" % (a, u), tag="scl%d" % a, align_bytes=64)
+        def rg_extra(u):
+            e = extra(u)
+            if e == 0:
+                return
+            c, s = chunk_of[u]
+            bank = psum.tile([P, 2, e * PACK], BF16, name="rgx_%d" % u, tag="bank")
+            for a in range(2):
+                pe_regroup(bank[:, a, :], raw_xh[c][:, a, :, s * UNIT:s * UNIT + e])
+            nc.scalar.copy(out=grp_xh[u][:, :, 0:e, :].rearrange("p a n t -> p a (n t)"), in_=bank[:])
+
+        def q_h1(u):
+            cd = codp.tile([P, UNIT], U32, name="codh1_%d" % u, tag="codh1", align_bytes=64)
+            sc = codp.tile([P, UNIT], U8, name="sclh1_%d" % u, tag="sclh1", align_bytes=64)
             nc.vector.quantize_mx(
-                out=cd[:].bitcast(FP8X4), scales=sc[:], in_=grp[(u, a)][:].rearrange("p n t -> p (n t)")
+                out=cd[:].bitcast(FP8X4), scales=sc[:], in_=grp_h1[u][:].rearrange("p n t -> p (n t)")
             )
-            codes[(u, a)] = (cd, sc)
+            cod_h1[u] = (cd, sc)
 
         def tanh(u, d, m0=0, m1=MT):
             if (u, d) not in tt:
@@ -121,17 +164,20 @@ def tile_mdlstmcellweights_pb_t_kernel(
         def mmsig(u, d, m):
             if (u, d) not in oo:
                 oo[(u, d)] = op.tile([P, MT, UNIT], F32, name="o%d_%d" % (d, u), tag="o%d" % d, bufs=(3 if d == 0 else 2))
-            xc, xs = codes[(u, 0)]
-            hc, hs = codes[(u, 1 + d)]
+            cd, sc = cod_xh[u]
+            if d == 0:
+                hc, hs = cd[:, 1], sc[:, 1]
+            else:
+                hc, hs = cod_h1[u][0][:], cod_h1[u][1][:]
             acc = psum.tile([P, UNIT], F32, name="acc%d_%d_%d" % (u, d, m), tag="bank")
             mc = slice(m * P, (m + 1) * P)
             nc.tensor.matmul_mx(
                 out=acc[:], lhsT=w_codes[0][:, mc].bitcast(FP8X4), lhsT_scale=w_scales[0][:, mc],
-                rhs=xc[:].bitcast(FP8X4), rhs_scale=xs[:], start=True, stop=False,
+                rhs=cd[:, 0].bitcast(FP8X4), rhs_scale=sc[:, 0], start=True, stop=False,
             )
             nc.tensor.matmul_mx(
                 out=acc[:], lhsT=w_codes[1][:, mc].bitcast(FP8X4), lhsT_scale=w_scales[1][:, mc],
-                rhs=hc[:].bitcast(FP8X4), rhs_scale=hs[:], start=False, stop=True,
+                rhs=hc.bitcast(FP8X4), rhs_scale=hs, start=False, stop=True,
             )
             nc.scalar.activation(out=oo[(u, d)][:, m, :], in_=acc[:], func=ACT.Sigmoid, bias=b_sb[:, m:m + 1], scale=1.0)
 
@@ -204,20 +250,20 @@ def tile_mdlstmcellweights_pb_t_kernel(
                 w_codes.append(wc)
                 w_scales.append(wsc)
 
+            new_xh(0)
             wq(0)
-            rgv(0, 0)
+            rg_one(0, 0)
             wq(1)
         op = ctx.enter_context(tc.tile_pool(name="op", bufs=2))
-        rgv(0, 1)
-        q(0, 0)
+        rg_one(0, 1)
+        q_one(0, 0)
         b_sb = const.tile([P, MT], F32, name="b_sb")
         nc.vector.tensor_copy(out=b_sb[:], in_=b_ps[:, 0:MT])
         ws_sb = const.tile([P, 2], F32, name="ws_sb")
         nc.vector.tensor_copy(out=ws_sb[:], in_=ws_bf[:])
-        rgs(0, 2, UNIT - SHARE[0], UNIT)
-        rgv(0, 2, 0, UNIT - SHARE[0])
-        q(0, 1)
-        q(0, 2)
+        rg_h1(0)
+        q_one(0, 1)
+        q_h1(0)
         if last_of_chunk(0) and next_m < n_chunks:
             for a in range(3):
                 ldm(next_m, a)
@@ -229,26 +275,24 @@ def tile_mdlstmcellweights_pb_t_kernel(
             has = v < N_UNITS
             last = u == N_UNITS - 1
             if has:
-                rgv(v, 0)
-                rgv(v, 1)
-                q(v, 0)
-                rgv(v, 2, 0, UNIT - SHARE[v])
-                q(v, 1)
+                new_xh(v)
+                rg_extra(v)
+                rg_both(v)
             if not last:
                 for m in range(MT):
                     mmsig(u, 0, m)
             if has:
-                rgs(v, 2, UNIT - SHARE[v], UNIT)
+                rg_h1(v)
             if not last:
                 tanh(u, 1)
                 if last_of_chunk(u) and next_c < n_chunks:
                     for d in range(2):
                         ldc(next_c, d)
                     next_c += 1
-            if not last:
                 prod(u, 0)
             if has:
-                q(v, 2)
+                q_both(v)
+                q_h1(v)
                 if last_of_chunk(v) and next_m < n_chunks:
                     for a in range(3):
                         ldm(next_m, a)

@@ -22,8 +22,7 @@ NPOS = 4096
 UNIT = 512
 N_UNITS = NPOS // UNIT
 CHUNKS = (1, 1, 2, 2, 2)
-EXTRA = 64
-EXTRA_FROM = 2
+SHARE = (512, 512, 512, 512, 512, 512, 512, 512)
 
 
 def tile_mdlstmcellweights_pb_t_kernel(
@@ -53,26 +52,18 @@ def tile_mdlstmcellweights_pb_t_kernel(
         def last_of_chunk(u):
             return u + 1 >= N_UNITS or chunk_of[u + 1][0] != chunk_of[u][0]
 
-        raw_xh = {}
-        raw_h1 = {}
+        raw_mov = {}
         raw_ct = {}
-        grp_xh = {}
-        grp_h1 = {}
-        cod_xh = {}
-        cod_h1 = {}
+        grp = {}
+        codes = {}
         tt = {}
         oo = {}
 
         def ldm(c, a):
             w = CHUNKS[c] * UNIT
-            src = mov_views[a][:, :, chunk_start[c]:chunk_start[c] + w]
-            if a == 2:
-                raw_h1[c] = rawp.tile([P, PACK, w], BF16, name="rawh1_%d" % c, tag="rawh1")
-                nc.sync.dma_start(out=raw_h1[c][:], in_=src)
-            else:
-                if c not in raw_xh:
-                    raw_xh[c] = rawp.tile([P, 2, PACK, w], BF16, name="rawxh_%d" % c, tag="rawxh")
-                nc.sync.dma_start(out=raw_xh[c][:, a], in_=src)
+            r = rawp.tile([P, PACK, w], BF16, name="rawm%d_%d" % (a, c), tag="rawm%d" % a)
+            nc.sync.dma_start(out=r[:], in_=mov_views[a][:, :, chunk_start[c]:chunk_start[c] + w])
+            raw_mov[(c, a)] = r
 
         def ldc(c, d):
             w = CHUNKS[c] * UNIT
@@ -80,78 +71,45 @@ def tile_mdlstmcellweights_pb_t_kernel(
             nc.sync.dma_start(out=r[:], in_=ct_views[d][:, :, chunk_start[c]:chunk_start[c] + w])
             raw_ct[(c, d)] = r
 
-        def extra(u):
-            return EXTRA if u >= EXTRA_FROM else 0
-
-        def new_xh(u):
-            grp_xh[u] = grpp.tile([P, 2, UNIT, PACK], BF16, name="grpxh_%d" % u, tag="grpxh", align_bytes=64)
-            cd = codp.tile([P, 2, UNIT], U32, name="codxh_%d" % u, tag="codxh", align_bytes=64)
-            sc = codp.tile([P, 2, UNIT], U8, name="sclxh_%d" % u, tag="sclxh", align_bytes=64)
-            cod_xh[u] = (cd, sc)
-
-        def rg_one(u, a):
+        def rg(copy_fn, u, a, c0, c1):
+            if c1 <= c0:
+                return
+            if (u, a) not in grp:
+                grp[(u, a)] = grpp.tile([P, UNIT, PACK], BF16, name="grp%d_%d" % (a, u), tag="grp%d" % a, align_bytes=64)
             c, s = chunk_of[u]
-            nc.vector.tensor_copy(
-                out=grp_xh[u][:, a].rearrange("p (c i) t -> p c t i", i=4),
-                in_=raw_xh[c][:, a, :, s * UNIT:(s + 1) * UNIT].rearrange("p t (c i) -> p c t i", i=4),
+            src = raw_mov[(c, a)][:, :, s * UNIT + c0:s * UNIT + c1]
+            copy_fn(
+                out=grp[(u, a)][:, c0:c1, :].rearrange("p (c i) t -> p c t i", i=4),
+                in_=src.rearrange("p t (c i) -> p c t i", i=4),
             )
 
-        def rg_both(u):
-            c, s = chunk_of[u]
-            e = extra(u)
-            nc.vector.tensor_copy(
-                out=grp_xh[u][:, :, e:, :].rearrange("p a (c i) t -> p a c t i", i=4),
-                in_=raw_xh[c][:, :, :, s * UNIT + e:(s + 1) * UNIT].rearrange("p a t (c i) -> p a c t i", i=4),
-            )
+        def rgv(u, a, c0=0, c1=UNIT):
+            rg(nc.vector.tensor_copy, u, a, c0, c1)
 
-        def q_one(u, a):
-            cd, sc = cod_xh[u]
-            nc.vector.quantize_mx(
-                out=cd[:, a].bitcast(FP8X4), scales=sc[:, a], in_=grp_xh[u][:, a].rearrange("p n t -> p (n t)")
-            )
-
-        def q_both(u):
-            cd, sc = cod_xh[u]
-            nc.vector.quantize_mx(
-                out=cd[:].rearrange("p a n -> p (a n)").bitcast(FP8X4),
-                scales=sc[:].rearrange("p a n -> p (a n)"),
-                in_=grp_xh[u][:].rearrange("p a n t -> p (a n t)"),
-            )
-
-        def pe_regroup(bank_cols, raw_tn):
-            nc.tensor.matmul(
-                out=bank_cols.rearrange("p (n t) -> p t n", t=PACK), lhsT=ident[:], rhs=raw_tn, start=True, stop=True
-            )
-
-        def rg_h1(u):
-            grp_h1[u] = grpp.tile([P, UNIT, PACK], BF16, name="grph1_%d" % u, tag="grph1", align_bytes=64)
+        def rgs(u, a, c0, c1):
+            assert c0 == 0 and c1 == UNIT
+            grp[(u, a)] = grpp.tile([P, UNIT, PACK], BF16, name="grp%d_%d" % (a, u), tag="grp%d" % a, align_bytes=64)
             c, s = chunk_of[u]
             for hf in range(2):
-                bank = psum.tile([P, 2 * P * PACK], BF16, name="rgb_%d_%d" % (u, hf), tag="bank")
+                bank = psum.tile([P, 2 * P * PACK], BF16, name="rgb%d_%d_%d" % (a, u, hf), tag="bank")
                 for qq in range(2):
                     n0 = s * UNIT + (2 * hf + qq) * P
-                    pe_regroup(bank[:, qq * P * PACK:(qq + 1) * P * PACK], raw_h1[c][:, :, n0:n0 + P])
+                    nc.tensor.matmul(
+                        out=bank[:, qq * P * PACK:(qq + 1) * P * PACK].rearrange("p (n t) -> p t n", t=PACK),
+                        lhsT=ident[:], rhs=raw_mov[(c, a)][:, :, n0:n0 + P], start=True, stop=True,
+                    )
                 nc.scalar.copy(
-                    out=grp_h1[u][:, 2 * hf * P:2 * (hf + 1) * P, :].rearrange("p n t -> p (n t)"), in_=bank[:]
+                    out=grp[(u, a)][:, 2 * hf * P:2 * (hf + 1) * P, :].rearrange("p n t -> p (n t)").bitcast(F32),
+                    in_=bank[:].bitcast(F32),
                 )
 
-        def rg_extra(u):
-            e = extra(u)
-            if e == 0:
-                return
-            c, s = chunk_of[u]
-            bank = psum.tile([P, 2, e * PACK], BF16, name="rgx_%d" % u, tag="bank")
-            for a in range(2):
-                pe_regroup(bank[:, a, :], raw_xh[c][:, a, :, s * UNIT:s * UNIT + e])
-            nc.scalar.copy(out=grp_xh[u][:, :, 0:e, :].rearrange("p a n t -> p a (n t)"), in_=bank[:])
-
-        def q_h1(u):
-            cd = codp.tile([P, UNIT], U32, name="codh1_%d" % u, tag="codh1", align_bytes=64)
-            sc = codp.tile([P, UNIT], U8, name="sclh1_%d" % u, tag="sclh1", align_bytes=64)
+        def q(u, a):
+            cd = codp.tile([P, UNIT], U32, name="cod%d_%d" % (a, u), tag="cod%d" % a, align_bytes=64)
+            sc = codp.tile([P, UNIT], U8, name="scl%d_%d" % (a, u), tag="scl%d" % a, align_bytes=64)
             nc.vector.quantize_mx(
-                out=cd[:].bitcast(FP8X4), scales=sc[:], in_=grp_h1[u][:].rearrange("p n t -> p (n t)")
+                out=cd[:].bitcast(FP8X4), scales=sc[:], in_=grp[(u, a)][:].rearrange("p n t -> p (n t)")
             )
-            cod_h1[u] = (cd, sc)
+            codes[(u, a)] = (cd, sc)
 
         def tanh(u, d, m0=0, m1=MT):
             if (u, d) not in tt:
@@ -164,20 +122,17 @@ def tile_mdlstmcellweights_pb_t_kernel(
         def mmsig(u, d, m):
             if (u, d) not in oo:
                 oo[(u, d)] = op.tile([P, MT, UNIT], F32, name="o%d_%d" % (d, u), tag="o%d" % d, bufs=(3 if d == 0 else 2))
-            cd, sc = cod_xh[u]
-            if d == 0:
-                hc, hs = cd[:, 1], sc[:, 1]
-            else:
-                hc, hs = cod_h1[u][0][:], cod_h1[u][1][:]
+            xc, xs = codes[(u, 0)]
+            hc, hs = codes[(u, 1 + d)]
             acc = psum.tile([P, UNIT], F32, name="acc%d_%d_%d" % (u, d, m), tag="bank")
             mc = slice(m * P, (m + 1) * P)
             nc.tensor.matmul_mx(
                 out=acc[:], lhsT=w_codes[0][:, mc].bitcast(FP8X4), lhsT_scale=w_scales[0][:, mc],
-                rhs=cd[:, 0].bitcast(FP8X4), rhs_scale=sc[:, 0], start=True, stop=False,
+                rhs=xc[:].bitcast(FP8X4), rhs_scale=xs[:], start=True, stop=False,
             )
             nc.tensor.matmul_mx(
                 out=acc[:], lhsT=w_codes[1][:, mc].bitcast(FP8X4), lhsT_scale=w_scales[1][:, mc],
-                rhs=hc.bitcast(FP8X4), rhs_scale=hs, start=False, stop=True,
+                rhs=hc[:].bitcast(FP8X4), rhs_scale=hs[:], start=False, stop=True,
             )
             nc.scalar.activation(out=oo[(u, d)][:, m, :], in_=acc[:], func=ACT.Sigmoid, bias=b_sb[:, m:m + 1], scale=1.0)
 
@@ -250,20 +205,20 @@ def tile_mdlstmcellweights_pb_t_kernel(
                 w_codes.append(wc)
                 w_scales.append(wsc)
 
-            new_xh(0)
             wq(0)
-            rg_one(0, 0)
+            rgv(0, 0)
             wq(1)
         op = ctx.enter_context(tc.tile_pool(name="op", bufs=2))
-        rg_one(0, 1)
-        q_one(0, 0)
+        rgv(0, 1)
+        q(0, 0)
         b_sb = const.tile([P, MT], F32, name="b_sb")
         nc.vector.tensor_copy(out=b_sb[:], in_=b_ps[:, 0:MT])
         ws_sb = const.tile([P, 2], F32, name="ws_sb")
         nc.vector.tensor_copy(out=ws_sb[:], in_=ws_bf[:])
-        rg_h1(0)
-        q_one(0, 1)
-        q_h1(0)
+        rgs(0, 2, UNIT - SHARE[0], UNIT)
+        rgv(0, 2, 0, UNIT - SHARE[0])
+        q(0, 1)
+        q(0, 2)
         if last_of_chunk(0) and next_m < n_chunks:
             for a in range(3):
                 ldm(next_m, a)
@@ -275,24 +230,26 @@ def tile_mdlstmcellweights_pb_t_kernel(
             has = v < N_UNITS
             last = u == N_UNITS - 1
             if has:
-                new_xh(v)
-                rg_extra(v)
-                rg_both(v)
+                rgv(v, 0)
+                rgv(v, 1)
+                q(v, 0)
+                rgv(v, 2, 0, UNIT - SHARE[v])
+                q(v, 1)
             if not last:
                 for m in range(MT):
                     mmsig(u, 0, m)
             if has:
-                rg_h1(v)
+                rgs(v, 2, UNIT - SHARE[v], UNIT)
             if not last:
                 tanh(u, 1)
                 if last_of_chunk(u) and next_c < n_chunks:
                     for d in range(2):
                         ldc(next_c, d)
                     next_c += 1
+            if not last:
                 prod(u, 0)
             if has:
-                q_both(v)
-                q_h1(v)
+                q(v, 2)
                 if last_of_chunk(v) and next_m < n_chunks:
                     for a in range(3):
                         ldm(next_m, a)

@@ -16,13 +16,15 @@ ALU = mybir.AluOpType
 
 P = 128
 PACK = 4
-CH = 512
+CH = P * PACK
 MT = CH // P
 NPOS = 4096
 UNIT = 512
 N_UNITS = NPOS // UNIT
 CHUNKS = (1, 1, 2, 2, 2)
-SHARE = (512, 512, 512, 512, 512, 512, 512, 512)
+X = 0
+H0 = 1
+H1 = 2
 
 
 def tile_mdlstmcellweights_pb_t_kernel(
@@ -36,6 +38,7 @@ def tile_mdlstmcellweights_pb_t_kernel(
         codp = ctx.enter_context(tc.tile_pool(name="codp", bufs=3))
         tp = ctx.enter_context(tc.tile_pool(name="tp", bufs=2))
         psum = ctx.enter_context(tc.psum_pool(name="psum", bufs=8))
+        ctx.enter_context(tc.manual_schedule())
 
         mov_views = [a.rearrange("(t p) n -> p t n", p=P) for a in (x, h_prev_dim0, h_prev_dim1)]
         ct_views = [a.rearrange("(m p) n -> p m n", p=P) for a in (ct0, ct1)]
@@ -43,9 +46,9 @@ def tile_mdlstmcellweights_pb_t_kernel(
 
         chunk_of = []
         chunk_start = []
-        for c, w in enumerate(CHUNKS):
+        for c, width in enumerate(CHUNKS):
             chunk_start.append(len(chunk_of) * UNIT)
-            for i in range(w):
+            for i in range(width):
                 chunk_of.append((c, i))
         n_chunks = len(CHUNKS)
 
@@ -54,103 +57,104 @@ def tile_mdlstmcellweights_pb_t_kernel(
 
         raw_mov = {}
         raw_ct = {}
-        grp = {}
+        grouped = {}
         codes = {}
-        tt = {}
-        oo = {}
+        tanh_ct = {}
+        gate = {}
 
-        def ldm(c, a):
+        def load_moving(c, a):
             w = CHUNKS[c] * UNIT
             r = rawp.tile([P, PACK, w], BF16, name="rawm%d_%d" % (a, c), tag="rawm%d" % a)
             nc.sync.dma_start(out=r[:], in_=mov_views[a][:, :, chunk_start[c]:chunk_start[c] + w])
             raw_mov[(c, a)] = r
 
-        def ldc(c, d):
+        def load_ct(c, d):
             w = CHUNKS[c] * UNIT
             r = rawp.tile([P, MT, w], BF16, name="rawc%d_%d" % (d, c), tag="rawc%d" % d)
             nc.sync.dma_start(out=r[:], in_=ct_views[d][:, :, chunk_start[c]:chunk_start[c] + w])
             raw_ct[(c, d)] = r
 
-        def rg(copy_fn, u, a, c0, c1):
-            if c1 <= c0:
-                return
-            if (u, a) not in grp:
-                grp[(u, a)] = grpp.tile([P, UNIT, PACK], BF16, name="grp%d_%d" % (a, u), tag="grp%d" % a, align_bytes=64)
-            c, s = chunk_of[u]
-            src = raw_mov[(c, a)][:, :, s * UNIT + c0:s * UNIT + c1]
-            copy_fn(
-                out=grp[(u, a)][:, c0:c1, :].rearrange("p (c i) t -> p c t i", i=4),
-                in_=src.rearrange("p t (c i) -> p c t i", i=4),
+        def new_grouped(u, a):
+            grouped[(u, a)] = grpp.tile(
+                [P, UNIT, PACK], BF16, name="grp%d_%d" % (a, u), tag="grp%d" % a, align_bytes=64
             )
 
-        def rgv(u, a, c0=0, c1=UNIT):
-            rg(nc.vector.tensor_copy, u, a, c0, c1)
-
-        def rgs(u, a, c0, c1):
-            assert c0 == 0 and c1 == UNIT
-            grp[(u, a)] = grpp.tile([P, UNIT, PACK], BF16, name="grp%d_%d" % (a, u), tag="grp%d" % a, align_bytes=64)
+        def regroup_on_vector(u, a):
+            new_grouped(u, a)
             c, s = chunk_of[u]
-            for hf in range(2):
-                bank = psum.tile([P, 2 * P * PACK], BF16, name="rgb%d_%d_%d" % (a, u, hf), tag="bank")
-                for qq in range(2):
-                    n0 = s * UNIT + (2 * hf + qq) * P
+            nc.vector.tensor_copy(
+                out=grouped[(u, a)][:].rearrange("p (c i) t -> p c t i", i=4),
+                in_=raw_mov[(c, a)][:, :, s * UNIT:(s + 1) * UNIT].rearrange("p t (c i) -> p c t i", i=4),
+            )
+
+        def regroup_on_tensor_engine(u, a):
+            new_grouped(u, a)
+            c, s = chunk_of[u]
+            for half in range(2):
+                bank = psum.tile([P, 2 * P * PACK], BF16, name="rgb%d_%d_%d" % (a, u, half), tag="bank")
+                for quarter in range(2):
+                    n0 = s * UNIT + (2 * half + quarter) * P
                     nc.tensor.matmul(
-                        out=bank[:, qq * P * PACK:(qq + 1) * P * PACK].rearrange("p (n t) -> p t n", t=PACK),
+                        out=bank[:, quarter * P * PACK:(quarter + 1) * P * PACK].rearrange("p (n t) -> p t n", t=PACK),
                         lhsT=ident[:], rhs=raw_mov[(c, a)][:, :, n0:n0 + P], start=True, stop=True,
                     )
                 nc.scalar.copy(
-                    out=grp[(u, a)][:, 2 * hf * P:2 * (hf + 1) * P, :].rearrange("p n t -> p (n t)").bitcast(F32),
-                    in_=bank[:].bitcast(F32),
+                    out=grouped[(u, a)][:, 2 * half * P:2 * (half + 1) * P, :].rearrange("p n t -> p (n t)"),
+                    in_=bank[:],
                 )
 
-        def q(u, a):
-            cd = codp.tile([P, UNIT], U32, name="cod%d_%d" % (a, u), tag="cod%d" % a, align_bytes=64)
-            sc = codp.tile([P, UNIT], U8, name="scl%d_%d" % (a, u), tag="scl%d" % a, align_bytes=64)
+        def quantise(u, a):
+            words = codp.tile([P, UNIT], U32, name="cod%d_%d" % (a, u), tag="cod%d" % a, align_bytes=64)
+            scales = codp.tile([P, UNIT], U8, name="scl%d_%d" % (a, u), tag="scl%d" % a, align_bytes=64)
             nc.vector.quantize_mx(
-                out=cd[:].bitcast(FP8X4), scales=sc[:], in_=grp[(u, a)][:].rearrange("p n t -> p (n t)")
+                out=words[:].bitcast(FP8X4), scales=scales[:], in_=grouped[(u, a)][:].rearrange("p n t -> p (n t)")
             )
-            codes[(u, a)] = (cd, sc)
+            codes[(u, a)] = (words, scales)
 
         def tanh(u, d, m0=0, m1=MT):
-            if (u, d) not in tt:
-                tt[(u, d)] = tp.tile([P, MT, UNIT], F32, name="t%d_%d" % (d, u), tag="t%d" % d)
+            if (u, d) not in tanh_ct:
+                tanh_ct[(u, d)] = tp.tile([P, MT, UNIT], F32, name="t%d_%d" % (d, u), tag="t%d" % d)
             c, s = chunk_of[u]
             nc.scalar.activation(
-                out=tt[(u, d)][:, m0:m1, :], in_=raw_ct[(c, d)][:, m0:m1, s * UNIT:(s + 1) * UNIT], func=ACT.Tanh
+                out=tanh_ct[(u, d)][:, m0:m1, :], in_=raw_ct[(c, d)][:, m0:m1, s * UNIT:(s + 1) * UNIT], func=ACT.Tanh
             )
 
-        def mmsig(u, d, m):
-            if (u, d) not in oo:
-                oo[(u, d)] = op.tile([P, MT, UNIT], F32, name="o%d_%d" % (d, u), tag="o%d" % d, bufs=(3 if d == 0 else 2))
-            xc, xs = codes[(u, 0)]
-            hc, hs = codes[(u, 1 + d)]
+        def gate_tile(u, d, m):
+            if (u, d) not in gate:
+                gate[(u, d)] = op.tile(
+                    [P, MT, UNIT], F32, name="o%d_%d" % (d, u), tag="o%d" % d, bufs=(3 if d == 0 else 2)
+                )
+            x_words, x_scales = codes[(u, X)]
+            h_words, h_scales = codes[(u, H0 + d)]
             acc = psum.tile([P, UNIT], F32, name="acc%d_%d_%d" % (u, d, m), tag="bank")
-            mc = slice(m * P, (m + 1) * P)
+            cols = slice(m * P, (m + 1) * P)
             nc.tensor.matmul_mx(
-                out=acc[:], lhsT=w_codes[0][:, mc].bitcast(FP8X4), lhsT_scale=w_scales[0][:, mc],
-                rhs=xc[:].bitcast(FP8X4), rhs_scale=xs[:], start=True, stop=False,
+                out=acc[:], lhsT=w_words[0][:, cols].bitcast(FP8X4), lhsT_scale=w_scales[0][:, cols],
+                rhs=x_words[:].bitcast(FP8X4), rhs_scale=x_scales[:], start=True, stop=False,
             )
             nc.tensor.matmul_mx(
-                out=acc[:], lhsT=w_codes[1][:, mc].bitcast(FP8X4), lhsT_scale=w_scales[1][:, mc],
-                rhs=hc[:].bitcast(FP8X4), rhs_scale=hs[:], start=False, stop=True,
+                out=acc[:], lhsT=w_words[1][:, cols].bitcast(FP8X4), lhsT_scale=w_scales[1][:, cols],
+                rhs=h_words[:].bitcast(FP8X4), rhs_scale=h_scales[:], start=False, stop=True,
             )
-            nc.scalar.activation(out=oo[(u, d)][:, m, :], in_=acc[:], func=ACT.Sigmoid, bias=b_sb[:, m:m + 1], scale=1.0)
+            nc.scalar.activation(
+                out=gate[(u, d)][:, m, :], in_=acc[:], func=ACT.Sigmoid, bias=b_sb[:, m:m + 1], scale=1.0
+            )
 
         def flat(t, m0, m1):
             return t[:, m0:m1, :].rearrange("p m n -> p (m n)")
 
-        def prod(u, d, m0=0, m1=MT):
-            of = flat(oo[(u, d)], m0, m1)
+        def product(u, d, m0=0, m1=MT):
+            o = flat(gate[(u, d)], m0, m1)
             nc.vector.scalar_tensor_tensor(
-                out=of, in0=of, scalar=ws_sb[:, d:d + 1], in1=flat(tt[(u, d)], m0, m1), op0=ALU.mult, op1=ALU.mult
+                out=o, in0=o, scalar=ws_sb[:, d:d + 1], in1=flat(tanh_ct[(u, d)], m0, m1), op0=ALU.mult, op1=ALU.mult
             )
 
         def add(u, m0=0, m1=MT):
-            of = flat(oo[(u, 0)], m0, m1)
-            nc.vector.tensor_tensor(out=of, in0=of, in1=flat(oo[(u, 1)], m0, m1), op=ALU.add)
+            o = flat(gate[(u, 0)], m0, m1)
+            nc.vector.tensor_tensor(out=o, in0=o, in1=flat(gate[(u, 1)], m0, m1), op=ALU.add)
 
-        def st(u, m0=0, m1=MT):
-            nc.sync.dma_start(out=out_v[:, m0:m1, u * UNIT:(u + 1) * UNIT], in_=oo[(u, 0)][:, m0:m1, :])
+        def store(u, m0=0, m1=MT):
+            nc.sync.dma_start(out=out_v[:, m0:m1, u * UNIT:(u + 1) * UNIT], in_=gate[(u, 0)][:, m0:m1, :])
 
         warm = const.tile([P, 1], F32, name="warm")
         nc.vector.memset(warm[:], 0.0)
@@ -168,18 +172,18 @@ def tile_mdlstmcellweights_pb_t_kernel(
             for wi in range(2):
                 w_raws.append(wtmp.tile([P, MT, CH], BF16, name="w_raw%d" % wi))
             nc.sync.dma_start(out=w_raws[0][:], in_=w_io.rearrange("(m p) k -> p m k", p=P))
-            ldc(0, 0)
-            ldm(0, 0)
+            load_ct(0, 0)
+            load_moving(0, X)
             nc.sync.dma_start(out=w_raws[1][:], in_=w_ho.rearrange("(m p) k -> p m k", p=P))
-            ldm(0, 1)
-            ldc(0, 1)
-            ldm(0, 2)
-            for a in range(3):
-                ldm(1, a)
+            load_moving(0, H0)
+            load_ct(0, 1)
+            load_moving(0, H1)
+            for a in (X, H0, H1):
+                load_moving(1, a)
             for d in range(2):
-                ldc(1, d)
-            next_m = 2
-            next_c = 2
+                load_ct(1, d)
+            next_moving = 2
+            next_ct = 2
 
             w_grps = []
             for wi in range(2):
@@ -190,85 +194,81 @@ def tile_mdlstmcellweights_pb_t_kernel(
                         nc.tensor.transpose(wt[:, t, :], w_raws[wi][:, m, t * P:(t + 1) * P], ident[:])
                     nc.scalar.copy(out=w_grp[:, m], in_=wt[:].rearrange("p t o -> p o t"))
                 w_grps.append(w_grp)
+                if wi == 0:
+                    tanh(0, 0)
             b_ps = psum.tile([P, P], BF16, name="b_ps", tag="bank")
             nc.tensor.transpose(b_ps[:], b_rows[:], ident[:])
 
-            w_codes = []
+            w_words = []
             w_scales = []
 
-            def wq(wi):
-                wc = const.tile([P, MT * P], U32, name="w_codes%d" % wi, align_bytes=64)
-                wsc = const.tile([P, MT * P], U8, name="w_scales%d" % wi, align_bytes=64)
+            def quantise_weights(wi):
+                words = const.tile([P, MT * P], U32, name="w_codes%d" % wi, align_bytes=64)
+                scales = const.tile([P, MT * P], U8, name="w_scales%d" % wi, align_bytes=64)
                 nc.vector.quantize_mx(
-                    out=wc[:].bitcast(FP8X4), scales=wsc[:], in_=w_grps[wi][:].rearrange("p m o t -> p (m o t)")
+                    out=words[:].bitcast(FP8X4), scales=scales[:], in_=w_grps[wi][:].rearrange("p m o t -> p (m o t)")
                 )
-                w_codes.append(wc)
-                w_scales.append(wsc)
+                w_words.append(words)
+                w_scales.append(scales)
 
-            wq(0)
-            rgv(0, 0)
-            wq(1)
+            regroup_on_vector(0, X)
+            quantise_weights(0)
+            regroup_on_vector(0, H0)
+            quantise(0, X)
+            quantise(0, H0)
+            quantise_weights(1)
         op = ctx.enter_context(tc.tile_pool(name="op", bufs=2))
-        rgv(0, 1)
-        q(0, 0)
+
         b_sb = const.tile([P, MT], F32, name="b_sb")
         nc.vector.tensor_copy(out=b_sb[:], in_=b_ps[:, 0:MT])
         ws_sb = const.tile([P, 2], F32, name="ws_sb")
         nc.vector.tensor_copy(out=ws_sb[:], in_=ws_bf[:])
-        rgs(0, 2, UNIT - SHARE[0], UNIT)
-        rgv(0, 2, 0, UNIT - SHARE[0])
-        q(0, 1)
-        q(0, 2)
-        if last_of_chunk(0) and next_m < n_chunks:
-            for a in range(3):
-                ldm(next_m, a)
-            next_m += 1
-        tanh(0, 0)
+        tanh(0, 1)
+        regroup_on_tensor_engine(0, H1)
+        for a in (X, H0, H1):
+            load_moving(next_moving, a)
+        next_moving += 1
+        regroup_on_vector(1, X)
+        quantise(0, H1)
+        regroup_on_vector(1, H0)
+        quantise(1, X)
+        quantise(1, H0)
 
-        for u in range(N_UNITS):
+        for u in range(N_UNITS - 1):
             v = u + 1
-            has = v < N_UNITS
-            last = u == N_UNITS - 1
-            if has:
-                rgv(v, 0)
-                rgv(v, 1)
-                q(v, 0)
-                rgv(v, 2, 0, UNIT - SHARE[v])
-                q(v, 1)
-            if not last:
-                for m in range(MT):
-                    mmsig(u, 0, m)
-            if has:
-                rgs(v, 2, UNIT - SHARE[v], UNIT)
-            if not last:
+            if u > 0:
+                regroup_on_vector(v, X)
+                regroup_on_vector(v, H0)
+                quantise(v, X)
+                quantise(v, H0)
+            for m in range(MT):
+                gate_tile(u, 0, m)
+            if u > 0:
                 tanh(u, 1)
-                if last_of_chunk(u) and next_c < n_chunks:
-                    for d in range(2):
-                        ldc(next_c, d)
-                    next_c += 1
-            if not last:
-                prod(u, 0)
-            if has:
-                q(v, 2)
-                if last_of_chunk(v) and next_m < n_chunks:
-                    for a in range(3):
-                        ldm(next_m, a)
-                    next_m += 1
-            if not last:
-                for m in range(MT):
-                    mmsig(u, 1, m)
-                if v < N_UNITS - 1:
-                    tanh(v, 0)
-                prod(u, 1)
-                add(u)
-                st(u)
-            else:
-                for m in range(MT):
-                    tanh(u, 0, m, m + 1)
-                    mmsig(u, 0, m)
-                    prod(u, 0, m, m + 1)
-                    tanh(u, 1, m, m + 1)
-                    mmsig(u, 1, m)
-                    prod(u, 1, m, m + 1)
-                    add(u, m, m + 1)
-                    st(u, m, m + 1)
+            regroup_on_tensor_engine(v, H1)
+            if last_of_chunk(u) and next_ct < n_chunks:
+                for d in range(2):
+                    load_ct(next_ct, d)
+                next_ct += 1
+            product(u, 0)
+            quantise(v, H1)
+            if last_of_chunk(v) and next_moving < n_chunks:
+                for a in (X, H0, H1):
+                    load_moving(next_moving, a)
+                next_moving += 1
+            for m in range(MT):
+                gate_tile(u, 1, m)
+            if v < N_UNITS - 1:
+                tanh(v, 0)
+            product(u, 1)
+            add(u)
+            store(u)
+
+        u = N_UNITS - 1
+        for m in range(MT):
+            for d in range(2):
+                tanh(u, d, m, m + 1)
+                gate_tile(u, d, m)
+                product(u, d, m, m + 1)
+            add(u, m, m + 1)
+            store(u, m, m + 1)

from contextlib import ExitStack

import concourse.mybir as mybir
from concourse.masks import make_identity

FLOPS = 3 * 2 * 512 * 512 * 4096

F32 = mybir.dt.float32
BF16 = mybir.dt.bfloat16
U32 = mybir.dt.uint32
U8 = mybir.dt.uint8
I32 = mybir.dt.int32
FP8X4 = mybir.dt.float8_e4m3fn_x4
ACT = mybir.ActivationFunctionType
ALU = mybir.AluOpType

P = 128
PACK = 4
CH = P * PACK
MT = CH // P
NPOS = 4096
UNIT = 512
N_UNITS = NPOS // UNIT
CHUNKS = (1, 1, 2, 2, 2)
X = 0
H0 = 1
H1 = 2


def tile_mdlstmcellweights_pb_t_kernel(
    tc, x, h_prev_dim0, h_prev_dim1, ct0, ct1, w_io, w_ho, b_o, weighted_sum, out
):
    nc = tc.nc
    with ExitStack() as ctx:
        const = ctx.enter_context(tc.tile_pool(name="const", bufs=1))
        rawp = ctx.enter_context(tc.tile_pool(name="rawp", bufs=2))
        grpp = ctx.enter_context(tc.tile_pool(name="grpp", bufs=2))
        codp = ctx.enter_context(tc.tile_pool(name="codp", bufs=3))
        tp = ctx.enter_context(tc.tile_pool(name="tp", bufs=2))
        psum = ctx.enter_context(tc.psum_pool(name="psum", bufs=8))
        ctx.enter_context(tc.manual_schedule())

        mov_views = [a.rearrange("(t p) n -> p t n", p=P) for a in (x, h_prev_dim0, h_prev_dim1)]
        ct_views = [a.rearrange("(m p) n -> p m n", p=P) for a in (ct0, ct1)]
        out_v = out.rearrange("(m p) n -> p m n", p=P)

        chunk_of = []
        chunk_start = []
        for c, width in enumerate(CHUNKS):
            chunk_start.append(len(chunk_of) * UNIT)
            for i in range(width):
                chunk_of.append((c, i))
        n_chunks = len(CHUNKS)

        def last_of_chunk(u):
            return u + 1 >= N_UNITS or chunk_of[u + 1][0] != chunk_of[u][0]

        raw_mov = {}
        raw_ct = {}
        grouped = {}
        codes = {}
        tanh_ct = {}
        gate = {}

        def load_moving(c, a):
            w = CHUNKS[c] * UNIT
            r = rawp.tile([P, PACK, w], BF16, name="rawm%d_%d" % (a, c), tag="rawm%d" % a)
            nc.sync.dma_start(out=r[:], in_=mov_views[a][:, :, chunk_start[c]:chunk_start[c] + w])
            raw_mov[(c, a)] = r

        def load_ct(c, d):
            w = CHUNKS[c] * UNIT
            r = rawp.tile([P, MT, w], BF16, name="rawc%d_%d" % (d, c), tag="rawc%d" % d)
            nc.sync.dma_start(out=r[:], in_=ct_views[d][:, :, chunk_start[c]:chunk_start[c] + w])
            raw_ct[(c, d)] = r

        def new_grouped(u, a):
            grouped[(u, a)] = grpp.tile(
                [P, UNIT, PACK], BF16, name="grp%d_%d" % (a, u), tag="grp%d" % a, align_bytes=64
            )

        def regroup_on_vector(u, a):
            new_grouped(u, a)
            c, s = chunk_of[u]
            nc.vector.tensor_copy(
                out=grouped[(u, a)][:].rearrange("p (c i) t -> p c t i", i=4),
                in_=raw_mov[(c, a)][:, :, s * UNIT:(s + 1) * UNIT].rearrange("p t (c i) -> p c t i", i=4),
            )

        def regroup_on_tensor_engine(u, a):
            new_grouped(u, a)
            c, s = chunk_of[u]
            for half in range(2):
                bank = psum.tile([P, 2 * P * PACK], BF16, name="rgb%d_%d_%d" % (a, u, half), tag="bank")
                for quarter in range(2):
                    n0 = s * UNIT + (2 * half + quarter) * P
                    nc.tensor.matmul(
                        out=bank[:, quarter * P * PACK:(quarter + 1) * P * PACK].rearrange("p (n t) -> p t n", t=PACK),
                        lhsT=ident[:], rhs=raw_mov[(c, a)][:, :, n0:n0 + P], start=True, stop=True,
                    )
                nc.scalar.copy(
                    out=grouped[(u, a)][:, 2 * half * P:2 * (half + 1) * P, :].rearrange("p n t -> p (n t)"),
                    in_=bank[:],
                )

        def quantise(u, a):
            words = codp.tile([P, UNIT], U32, name="cod%d_%d" % (a, u), tag="cod%d" % a, align_bytes=64)
            scales = codp.tile([P, UNIT], U8, name="scl%d_%d" % (a, u), tag="scl%d" % a, align_bytes=64)
            nc.vector.quantize_mx(
                out=words[:].bitcast(FP8X4), scales=scales[:], in_=grouped[(u, a)][:].rearrange("p n t -> p (n t)")
            )
            codes[(u, a)] = (words, scales)

        def tanh(u, d, m0=0, m1=MT):
            if (u, d) not in tanh_ct:
                tanh_ct[(u, d)] = tp.tile([P, MT, UNIT], F32, name="t%d_%d" % (d, u), tag="t%d" % d)
            c, s = chunk_of[u]
            nc.scalar.activation(
                out=tanh_ct[(u, d)][:, m0:m1, :], in_=raw_ct[(c, d)][:, m0:m1, s * UNIT:(s + 1) * UNIT], func=ACT.Tanh
            )

        def gate_tile(u, d, m):
            if (u, d) not in gate:
                gate[(u, d)] = op.tile(
                    [P, MT, UNIT], F32, name="o%d_%d" % (d, u), tag="o%d" % d, bufs=(3 if d == 0 else 2)
                )
            x_words, x_scales = codes[(u, X)]
            h_words, h_scales = codes[(u, H0 + d)]
            acc = psum.tile([P, UNIT], F32, name="acc%d_%d_%d" % (u, d, m), tag="bank")
            cols = slice(m * P, (m + 1) * P)
            nc.tensor.matmul_mx(
                out=acc[:], lhsT=w_words[0][:, cols].bitcast(FP8X4), lhsT_scale=w_scales[0][:, cols],
                rhs=x_words[:].bitcast(FP8X4), rhs_scale=x_scales[:], start=True, stop=False,
            )
            nc.tensor.matmul_mx(
                out=acc[:], lhsT=w_words[1][:, cols].bitcast(FP8X4), lhsT_scale=w_scales[1][:, cols],
                rhs=h_words[:].bitcast(FP8X4), rhs_scale=h_scales[:], start=False, stop=True,
            )
            nc.scalar.activation(
                out=gate[(u, d)][:, m, :], in_=acc[:], func=ACT.Sigmoid, bias=b_sb[:, m:m + 1], scale=1.0
            )

        def flat(t, m0, m1):
            return t[:, m0:m1, :].rearrange("p m n -> p (m n)")

        def product(u, d, m0=0, m1=MT):
            o = flat(gate[(u, d)], m0, m1)
            nc.vector.scalar_tensor_tensor(
                out=o, in0=o, scalar=ws_sb[:, d:d + 1], in1=flat(tanh_ct[(u, d)], m0, m1), op0=ALU.mult, op1=ALU.mult
            )

        def add(u, m0=0, m1=MT):
            o = flat(gate[(u, 0)], m0, m1)
            nc.vector.tensor_tensor(out=o, in0=o, in1=flat(gate[(u, 1)], m0, m1), op=ALU.add)

        def store(u, m0=0, m1=MT):
            nc.sync.dma_start(out=out_v[:, m0:m1, u * UNIT:(u + 1) * UNIT], in_=gate[(u, 0)][:, m0:m1, :])

        warm = const.tile([P, 1], F32, name="warm")
        nc.vector.memset(warm[:], 0.0)
        nc.scalar.activation(out=warm[:], in_=warm[:], func=ACT.Sigmoid)
        b_rows = const.tile([P, P], BF16, name="b_rows")
        nc.vector.memset(b_rows[:].bitcast(I32), 0)
        nc.scalar.dma_start(out=b_rows[0:MT, :], in_=b_o.rearrange("(m p) one -> m (p one)", p=P))
        ws_bf = const.tile([P, 2], BF16, name="ws_bf")
        nc.scalar.dma_start(out=ws_bf[:], in_=weighted_sum.partition_broadcast(P))
        ident = const.tile([P, P], BF16, name="ident")
        make_identity(nc, ident[:])

        with tc.tile_pool(name="wtmp", bufs=1) as wtmp:
            w_raws = []
            for wi in range(2):
                w_raws.append(wtmp.tile([P, MT, CH], BF16, name="w_raw%d" % wi))
            nc.sync.dma_start(out=w_raws[0][:], in_=w_io.rearrange("(m p) k -> p m k", p=P))
            load_ct(0, 0)
            load_moving(0, X)
            nc.sync.dma_start(out=w_raws[1][:], in_=w_ho.rearrange("(m p) k -> p m k", p=P))
            load_moving(0, H0)
            load_ct(0, 1)
            load_moving(0, H1)
            for a in (X, H0, H1):
                load_moving(1, a)
            for d in range(2):
                load_ct(1, d)
            next_moving = 2
            next_ct = 2

            w_grps = []
            for wi in range(2):
                w_grp = wtmp.tile([P, MT, P, PACK], BF16, name="w_grp%d" % wi, align_bytes=64)
                for m in range(MT):
                    wt = psum.tile([P, PACK, P], BF16, name="wt%d_%d" % (wi, m), tag="bank")
                    for t in range(PACK):
                        nc.tensor.transpose(wt[:, t, :], w_raws[wi][:, m, t * P:(t + 1) * P], ident[:])
                    nc.scalar.copy(out=w_grp[:, m], in_=wt[:].rearrange("p t o -> p o t"))
                w_grps.append(w_grp)
                if wi == 0:
                    tanh(0, 0)
            b_ps = psum.tile([P, P], BF16, name="b_ps", tag="bank")
            nc.tensor.transpose(b_ps[:], b_rows[:], ident[:])

            w_words = []
            w_scales = []

            def quantise_weights(wi):
                words = const.tile([P, MT * P], U32, name="w_codes%d" % wi, align_bytes=64)
                scales = const.tile([P, MT * P], U8, name="w_scales%d" % wi, align_bytes=64)
                nc.vector.quantize_mx(
                    out=words[:].bitcast(FP8X4), scales=scales[:], in_=w_grps[wi][:].rearrange("p m o t -> p (m o t)")
                )
                w_words.append(words)
                w_scales.append(scales)

            regroup_on_vector(0, X)
            quantise_weights(0)
            regroup_on_vector(0, H0)
            quantise(0, X)
            quantise(0, H0)
            quantise_weights(1)
        op = ctx.enter_context(tc.tile_pool(name="op", bufs=2))

        b_sb = const.tile([P, MT], F32, name="b_sb")
        nc.vector.tensor_copy(out=b_sb[:], in_=b_ps[:, 0:MT])
        ws_sb = const.tile([P, 2], F32, name="ws_sb")
        nc.vector.tensor_copy(out=ws_sb[:], in_=ws_bf[:])
        tanh(0, 1)
        regroup_on_tensor_engine(0, H1)
        for a in (X, H0, H1):
            load_moving(next_moving, a)
        next_moving += 1
        regroup_on_vector(1, X)
        quantise(0, H1)
        regroup_on_vector(1, H0)
        quantise(1, X)
        quantise(1, H0)

        for u in range(N_UNITS - 1):
            v = u + 1
            if u > 0:
                regroup_on_vector(v, X)
                regroup_on_vector(v, H0)
                quantise(v, X)
                quantise(v, H0)
            for m in range(MT):
                gate_tile(u, 0, m)
            if u > 0:
                tanh(u, 1)
            regroup_on_tensor_engine(v, H1)
            if last_of_chunk(u) and next_ct < n_chunks:
                for d in range(2):
                    load_ct(next_ct, d)
                next_ct += 1
            product(u, 0)
            quantise(v, H1)
            if last_of_chunk(v) and next_moving < n_chunks:
                for a in (X, H0, H1):
                    load_moving(next_moving, a)
                next_moving += 1
            for m in range(MT):
                gate_tile(u, 1, m)
            if v < N_UNITS - 1:
                tanh(v, 0)
            product(u, 1)
            add(u)
            store(u)

        u = N_UNITS - 1
        for m in range(MT):
            for d in range(2):
                tanh(u, d, m, m + 1)
                gate_tile(u, d, m)
                product(u, d, m, m + 1)
            add(u, m, m + 1)
            store(u, m, m + 1)
